import numpy as np
import ml_dtypes


def mxq(x, axis, fmt="e4m3"):
    dtype, down = {"e4m3": (ml_dtypes.float8_e4m3fn, 7), "e5m2": (ml_dtypes.float8_e5m2, 14)}[fmt]
    v = np.moveaxis(np.asarray(x, np.float32).astype(ml_dtypes.bfloat16).astype(np.float64), axis, -1)
    blocks = v.reshape(v.shape[:-1] + (-1, 32))
    amax = np.abs(blocks).max(-1, keepdims=True)
    byte = np.maximum(np.where(amax > 0, np.frexp(amax)[1] - 1 + 127, 0) - down, 1)
    scale = np.exp2(byte - 127.0)
    codes = (blocks / scale).astype(np.float32).astype(dtype).astype(np.float64)
    return np.moveaxis((codes * scale).reshape(v.shape), -1, axis)


WIDE = False


def mx_kscale(k):
    if not WIDE:
        return np.ones(k)
    levels = np.array([10, -10, 5, -5, 0])
    a = np.random.permutation(np.resize(levels, k // 512 * 4)).reshape(k // 512, 4)
    idx = np.arange(k)
    return np.exp2(a[idx // 512, idx % 128 // 32])


BF16 = ml_dtypes.bfloat16


def bf(x):
    return np.asarray(x, np.float32).astype(BF16)


def f64(x):
    return np.asarray(x).astype(np.float64)


B, Tq, Tk, C = 2, 64, 64, 512
C2 = 2 * C
VAR_EPS = 1e-6
LN_EPS = 1e-5


def layernorm(x, g, b):
    m = x.mean(-1, keepdims=True)
    v = ((x - m) ** 2).mean(-1, keepdims=True)
    return (x - m) / np.sqrt(v + LN_EPS) * g + b


def softplus(v):
    return np.log(1.0 + np.exp(v))


def setup_inputs():
    s = mx_kscale(C)
    w = 1.0 / np.sqrt(C)
    return {"context": bf(np.random.standard_normal((B, Tk, C)) * s),
            "eps_noise": bf(np.random.standard_normal((B, Tk, C))),
            "Wk": bf(np.random.standard_normal((C2, C)) * w / s),
            "bk": bf(np.random.standard_normal(C2) * 0.2),
            "Wv": bf(np.random.standard_normal((C2, C)) * w / s),
            "bv": bf(np.random.standard_normal(C2) * 0.2),
            "ln_k_g": bf(1.0 + 0.1 * np.random.standard_normal(C)),
            "ln_k_b": bf(np.random.standard_normal(C) * 0.2),
            "ln_v_g": bf(1.0 + 0.1 * np.random.standard_normal(C)),
            "ln_v_b": bf(np.random.standard_normal(C) * 0.2)}


def reference(context, eps_noise, Wk, bk, Wv, bv, ln_k_g, ln_k_b, ln_v_g, ln_v_b):
    cq = mxq(f64(context), 2, "e4m3")
    k_out = (cq @ mxq(f64(Wk), 1, "e4m3").T) + f64(bk)
    k_mu = layernorm(k_out[..., :C], f64(ln_k_g), f64(ln_k_b))
    k_var = softplus(k_out[..., C:]) + VAR_EPS
    v_out = (cq @ mxq(f64(Wv), 1, "e4m3").T) + f64(bv)
    v_mu = layernorm(v_out[..., :C], f64(ln_v_g), f64(ln_v_b))
    v_var = softplus(v_out[..., C:]) + VAR_EPS
    v_sample = v_mu + np.sqrt(v_var) * f64(eps_noise)
    return k_mu, k_var, v_sample

@@ -1,0 +1,218 @@
+from contextlib import ExitStack
+
+import concourse.mybir as mybir
+from concourse.masks import make_identity
+
+F32 = mybir.dt.float32
+BF16 = mybir.dt.bfloat16
+U32 = mybir.dt.uint32
+U8 = mybir.dt.uint8
+FP8X4 = mybir.dt.float8_e4m3fn_x4
+ALU = mybir.AluOpType
+ACT = mybir.ActivationFunctionType
+
+P = 128
+C = 512
+BANK = 512
+VAR_EPS = 1e-6
+LN_EPS = 1e-5
+
+FLOPS = 2 * P * C * 4 * C
+
+
+def transpose_words(nc, bank, first_column, rows_bf16, ident):
+    words = rows_bf16.bitcast(F32)
+    for u in range(2):
+        nc.tensor.transpose(
+            bank[:, first_column + P * u : first_column + P * (u + 1)],
+            words[:, P * u : P * (u + 1)],
+            ident[:],
+        )
+
+
+def rows_to_columns(nc, psum, keep, rows, n_rows, ident, name):
+    flipped = psum.tile([P, BANK], F32, tag="words", name=name + "_flipped")
+    nc.tensor.transpose(flipped[:, 0:P], rows[:].bitcast(F32), ident[:])
+    columns = keep.tile([P, n_rows], F32, name=name)
+    nc.vector.tensor_copy(out=columns[:], in_=flipped[:, 0:n_rows])
+    return columns
+
+
+def repeat_on_all_partitions(nc, bank, columns, first_row, ident):
+    for r in range(4):
+        nc.tensor.transpose(
+            bank[:, P * r : P * (r + 1)],
+            columns[:, first_row + r : first_row + r + 1].to_broadcast([P, P]),
+            ident[:],
+        )
+
+
+def layer_norm(nc, work, small, x, gain, shift, minus_half, name):
+    stats = small.tile([P, 6], F32, name=name + "_stats")
+    nc.vector.bn_stats(out=stats[:], in_=x[:])
+    mean_var = small.tile([P, 2], F32, name=name + "_mean_var")
+    nc.vector.bn_aggr(out=mean_var[:], in_=stats[:])
+    rstd = small.tile([P, 1], F32, name=name + "_rstd")
+    nc.gpsimd.tensor_scalar(
+        out=rstd[:], in0=mean_var[:, 1:2], scalar1=LN_EPS, scalar2=None, op0=ALU.add
+    )
+    nc.gpsimd.tensor_tensor(out=rstd[:], in0=rstd[:], in1=minus_half[:], op=ALU.pow)
+    centred = work.tile([P, C], F32, name=name + "_centred")
+    nc.vector.scalar_tensor_tensor(
+        out=centred[:], in0=x[:], scalar=mean_var[:, 0:1], in1=gain,
+        op0=ALU.subtract, op1=ALU.mult,
+    )
+    normed = work.tile([P, C], F32, name=name + "_normed")
+    nc.vector.scalar_tensor_tensor(
+        out=normed[:], in0=centred[:], scalar=rstd[:, 0:1], in1=shift,
+        op0=ALU.mult, op1=ALU.add,
+    )
+    return normed
+
+
+def tile_probcrossattention_pa_s_kernel(
+    tc, context, eps_noise, Wk, bk, Wv, bv, ln_k_g, ln_k_b, ln_v_g, ln_v_b, out_0, out_1, out_2
+):
+    nc = tc.nc
+    k_mu_out = out_0.flatten_outer_dims()
+    k_var_out = out_1.flatten_outer_dims()
+    v_sample_out = out_2.flatten_outer_dims()
+
+    V_VAR, K_VAR = 0, 1
+    chunks = ((Wv, C, 1), (Wk, C, 0), (Wv, 0, 1), (Wk, 0, 0))
+
+    with ExitStack() as stack:
+        keep = stack.enter_context(tc.tile_pool(name="keep", bufs=1))
+        small = stack.enter_context(tc.tile_pool(name="small", bufs=1))
+        work = stack.enter_context(tc.tile_pool(name="work", bufs=1))
+        psum = stack.enter_context(tc.psum_pool(name="psum", bufs=4))
+        psum_acc = stack.enter_context(tc.psum_pool(name="psum_acc", bufs=2))
+        psum_affine = stack.enter_context(tc.psum_pool(name="psum_affine", bufs=1))
+
+        ident = keep.tile([P, P], F32)
+        make_identity(nc, ident[:])
+        one = small.tile([P, 1], F32)
+        nc.vector.memset(one[:], 1.0)
+        minus_half = small.tile([P, 1], F32)
+        nc.vector.memset(minus_half[:], -0.5)
+
+        bias_rows = keep.tile([P, 2 * P], BF16)
+        nc.vector.memset(bias_rows[:], 0.0)
+        affine_rows = keep.tile([P, 2 * P], BF16)
+        nc.vector.memset(affine_rows[:], 0.0)
+        nc.scalar.dma_start(out=bias_rows[0:4, :], in_=bk.rearrange("(r c) -> r c", r=4))
+        nc.scalar.dma_start(out=bias_rows[4:8, :], in_=bv.rearrange("(r c) -> r c", r=4))
+
+        ctx_rows = keep.tile([P, C], BF16)
+        nc.sync.dma_start(out=ctx_rows[:], in_=context.flatten_outer_dims())
+        w_rows = []
+        for i, (w, first_row, bias_row) in enumerate(chunks):
+            w_tile = keep.tile([P, 2, 2, C], BF16, name="w_rows%d" % i)
+            nc.sync.dma_start(
+                out=w_tile[:],
+                in_=w[first_row : first_row + C, :].rearrange("(s p t) k -> p s t k", s=2, t=2),
+            )
+            w_rows.append(w_tile)
+        for i, vector in enumerate((ln_k_g, ln_k_b, ln_v_g, ln_v_b)):
+            nc.sync.dma_start(
+                out=affine_rows[2 * i : 2 * i + 2, :], in_=vector.rearrange("(r c) -> r c", r=2)
+            )
+        noise = keep.tile([P, C], BF16)
+        nc.sync.dma_start(out=noise[:], in_=eps_noise.flatten_outer_dims())
+
+        bias_columns = rows_to_columns(nc, psum, small, bias_rows, 8, ident, "bias_columns")
+        bias_all = keep.tile([P, 2, 2 * C], BF16)
+        for i in range(2):
+            bank = psum.tile([P, BANK], F32, tag="words", name="bias_bank%d" % i)
+            repeat_on_all_partitions(nc, bank, bias_columns, 4 * i, ident)
+            if i == 0:
+                nc.scalar.copy(out=bias_all[:, i, :].bitcast(F32), in_=bank[:])
+            else:
+                nc.vector.tensor_copy(out=bias_all[:, i, :].bitcast(F32), in_=bank[:])
+
+        ctx_bank = psum.tile([P, BANK], F32, tag="words")
+        transpose_words(nc, ctx_bank, 0, ctx_rows[:], ident)
+        ctx_grouped = keep.tile([P, 4 * P], BF16, align_bytes=64)
+        nc.vector.tensor_copy(
+            out=ctx_grouped[:].bitcast(F32).rearrange("p (n u) -> p n u", u=2),
+            in_=ctx_bank[:, 0 : 2 * P].rearrange("p (u n) -> p n u", u=2),
+        )
+        ctx_codes = keep.tile([P, P], U32, align_bytes=64)
+        ctx_scales = keep.tile([P, P], U8, align_bytes=64)
+        nc.vector.quantize_mx(
+            out=ctx_codes[:].bitcast(FP8X4), scales=ctx_scales[:], in_=ctx_grouped[:]
+        )
+
+        x_var = work.tile([P, 2, C], F32)
+        x_mu = [work.tile([P, C], F32, name="x_mu%d" % i) for i in range(2)]
+        x_of_chunk = (x_var[:, 0, :], x_var[:, 1, :], x_mu[0][:], x_mu[1][:])
+        for i, (w, first_row, bias_row) in enumerate(chunks):
+            grouped = keep.tile([P, 4 * C], BF16, align_bytes=64, name="grouped%d" % i)
+            for s in range(2):
+                bank = psum.tile([P, BANK], F32, tag="words", name="w_bank%d_%d" % (i, s))
+                for t in range(2):
+                    transpose_words(nc, bank, 2 * P * t, w_rows[i][:, s, t, :], ident)
+                source = bank[:].rearrange("p (t u n) -> p n t u", t=2, u=2)
+                target = grouped[:].bitcast(F32)[:, BANK * s : BANK * (s + 1)].rearrange(
+                    "p (n t u) -> p n t u", t=2, u=2
+                )
+                if s == 0:
+                    nc.scalar.copy(out=target, in_=source)
+                else:
+                    nc.vector.tensor_copy(out=target, in_=source)
+            w_codes = keep.tile([P, C], U32, align_bytes=64, name="w_codes%d" % i)
+            w_scales = keep.tile([P, C], U8, align_bytes=64, name="w_scales%d" % i)
+            nc.vector.quantize_mx(
+                out=w_codes[:].bitcast(FP8X4), scales=w_scales[:], in_=grouped[:]
+            )
+            acc = psum_acc.tile([P, C], F32)
+            nc.tensor.matmul_mx(
+                out=acc[:],
+                lhsT=ctx_codes[:].bitcast(FP8X4),
+                lhsT_scale=ctx_scales[:],
+                rhs=w_codes[:].bitcast(FP8X4),
+                rhs_scale=w_scales[:],
+                start=True,
+                stop=True,
+            )
+            nc.vector.tensor_tensor(
+                out=x_of_chunk[i], in0=acc[:],
+                in1=bias_all[:, bias_row, first_row : first_row + C], op=ALU.add,
+            )
+
+        shrunk = work.tile([P, 2, C], F32)
+        for half in (V_VAR, K_VAR):
+            nc.scalar.activation(out=shrunk[:, half, :], in_=x_var[:, half, :], func=ACT.Abs)
+            nc.scalar.activation(
+                out=shrunk[:, half, :], in_=shrunk[:, half, :], func=ACT.Exp, scale=-1.0
+            )
+        ramp = work.tile([P, 2, C], F32)
+        nc.vector.tensor_scalar(
+            out=ramp[:], in0=x_var[:], scalar1=0.0, scalar2=VAR_EPS, op0=ALU.max, op1=ALU.add
+        )
+        log_term = work.tile([P, 2, C], F32)
+        nc.scalar.activation(out=log_term[:], in_=shrunk[:], func=ACT.Ln, bias=one[:, 0:1])
+        variance = work.tile([P, 2, C], F32)
+        nc.vector.tensor_tensor(out=variance[:], in0=ramp[:], in1=log_term[:], op=ALU.add)
+        nc.sync.dma_start(out=k_var_out, in_=variance[:, K_VAR, :])
+        v_std = work.tile([P, C], F32)
+        nc.scalar.activation(out=v_std[:], in_=variance[:, V_VAR, :], func=ACT.Sqrt)
+
+        affine_columns = rows_to_columns(nc, psum, small, affine_rows, 8, ident, "affine_columns")
+        affine = []
+        for i in range(2):
+            bank = psum_affine.tile([P, BANK], F32, name="affine_bank%d" % i)
+            repeat_on_all_partitions(nc, bank, affine_columns, 4 * i, ident)
+            affine.append(bank[:].bitcast(BF16))
+
+        v_mu = layer_norm(
+            nc, work, small, x_mu[0], affine[1][:, 0:C], affine[1][:, C : 2 * C], minus_half, "v"
+        )
+        k_mu = layer_norm(
+            nc, work, small, x_mu[1], affine[0][:, 0:C], affine[0][:, C : 2 * C], minus_half, "k"
+        )
+        nc.sync.dma_start(out=k_mu_out, in_=k_mu[:])
+        v_sample = work.tile([P, C], F32)
+        nc.vector.tensor_tensor(out=v_sample[:], in0=v_std[:], in1=noise[:], op=ALU.mult)
+        nc.vector.tensor_tensor(out=v_sample[:], in0=v_sample[:], in1=v_mu[:], op=ALU.add)
+        nc.sync.dma_start(out=v_sample_out, in_=v_sample[:])

@@ -14,8 +14,15 @@ ACT = mybir.ActivationFunctionType
 P = 128
 C = 512
 BANK = 512
+PIECE = 256
+N_PIECES = 4 * C // PIECE
+N_VAR_PIECES = N_PIECES // 2
 VAR_EPS = 1e-6
 LN_EPS = 1e-5
+
+QUANTISE_LAG = 1
+MULTIPLY_LAG = 3
+EXP_LAG = 4
 
 FLOPS = 2 * P * C * 4 * C
 
@@ -30,44 +37,19 @@ def transpose_words(nc, bank, first_column, rows_bf16, ident):
         )
 
 
-def rows_to_columns(nc, psum, keep, rows, n_rows, ident, name):
+def rows_to_columns(nc, psum, small, rows, n_rows, ident, name):
     flipped = psum.tile([P, BANK], F32, tag="words", name=name + "_flipped")
     nc.tensor.transpose(flipped[:, 0:P], rows[:].bitcast(F32), ident[:])
-    columns = keep.tile([P, n_rows], F32, name=name)
+    columns = small.tile([P, n_rows], F32, name=name)
     nc.vector.tensor_copy(out=columns[:], in_=flipped[:, 0:n_rows])
     return columns
 
 
-def repeat_on_all_partitions(nc, bank, columns, first_row, ident):
-    for r in range(4):
+def repeat_on_all_partitions(nc, bank, columns, four_rows, ident):
+    for i, r in enumerate(four_rows):
         nc.tensor.transpose(
-            bank[:, P * r : P * (r + 1)],
-            columns[:, first_row + r : first_row + r + 1].to_broadcast([P, P]),
-            ident[:],
+            bank[:, P * i : P * (i + 1)], columns[:, r : r + 1].to_broadcast([P, P]), ident[:]
         )
-
-
-def layer_norm(nc, work, small, x, gain, shift, minus_half, name):
-    stats = small.tile([P, 6], F32, name=name + "_stats")
-    nc.vector.bn_stats(out=stats[:], in_=x[:])
-    mean_var = small.tile([P, 2], F32, name=name + "_mean_var")
-    nc.vector.bn_aggr(out=mean_var[:], in_=stats[:])
-    rstd = small.tile([P, 1], F32, name=name + "_rstd")
-    nc.gpsimd.tensor_scalar(
-        out=rstd[:], in0=mean_var[:, 1:2], scalar1=LN_EPS, scalar2=None, op0=ALU.add
-    )
-    nc.gpsimd.tensor_tensor(out=rstd[:], in0=rstd[:], in1=minus_half[:], op=ALU.pow)
-    centred = work.tile([P, C], F32, name=name + "_centred")
-    nc.vector.scalar_tensor_tensor(
-        out=centred[:], in0=x[:], scalar=mean_var[:, 0:1], in1=gain,
-        op0=ALU.subtract, op1=ALU.mult,
-    )
-    normed = work.tile([P, C], F32, name=name + "_normed")
-    nc.vector.scalar_tensor_tensor(
-        out=normed[:], in0=centred[:], scalar=rstd[:, 0:1], in1=shift,
-        op0=ALU.mult, op1=ALU.add,
-    )
-    return normed
 
 
 def tile_probcrossattention_pa_s_kernel(
@@ -78,57 +60,54 @@ def tile_probcrossattention_pa_s_kernel(
     k_var_out = out_1.flatten_outer_dims()
     v_sample_out = out_2.flatten_outer_dims()
 
-    V_VAR, K_VAR = 0, 1
-    chunks = ((Wv, C, 1), (Wk, C, 0), (Wv, 0, 1), (Wk, 0, 0))
+    piece_weights = []
+    piece_first_row = []
+    piece_bias_row = []
+    for w, bias_base, half in ((Wv, 4, 1), (Wk, 0, 1), (Wv, 4, 0), (Wk, 0, 0)):
+        for s in range(2):
+            piece_weights.append(w)
+            piece_first_row.append(C * half + PIECE * s)
+            piece_bias_row.append(bias_base + 2 * half + s)
 
     with ExitStack() as stack:
+        stack.enter_context(tc.manual_schedule())
         keep = stack.enter_context(tc.tile_pool(name="keep", bufs=1))
         small = stack.enter_context(tc.tile_pool(name="small", bufs=1))
-        work = stack.enter_context(tc.tile_pool(name="work", bufs=1))
         psum = stack.enter_context(tc.psum_pool(name="psum", bufs=4))
         psum_acc = stack.enter_context(tc.psum_pool(name="psum_acc", bufs=2))
         psum_affine = stack.enter_context(tc.psum_pool(name="psum_affine", bufs=1))
 
         ident = keep.tile([P, P], F32)
         make_identity(nc, ident[:])
+        bias_rows = keep.tile([P, 2 * P], BF16)
+        nc.vector.memset(bias_rows[:], 0.0)
+        affine_rows = keep.tile([P, 2 * P], BF16)
+        nc.vector.memset(affine_rows[:], 0.0)
         one = small.tile([P, 1], F32)
         nc.vector.memset(one[:], 1.0)
         minus_half = small.tile([P, 1], F32)
         nc.vector.memset(minus_half[:], -0.5)
 
-        bias_rows = keep.tile([P, 2 * P], BF16)
-        nc.vector.memset(bias_rows[:], 0.0)
-        affine_rows = keep.tile([P, 2 * P], BF16)
-        nc.vector.memset(affine_rows[:], 0.0)
-        nc.scalar.dma_start(out=bias_rows[0:4, :], in_=bk.rearrange("(r c) -> r c", r=4))
-        nc.scalar.dma_start(out=bias_rows[4:8, :], in_=bv.rearrange("(r c) -> r c", r=4))
-
         ctx_rows = keep.tile([P, C], BF16)
         nc.sync.dma_start(out=ctx_rows[:], in_=context.flatten_outer_dims())
-        w_rows = []
-        for i, (w, first_row, bias_row) in enumerate(chunks):
-            w_tile = keep.tile([P, 2, 2, C], BF16, name="w_rows%d" % i)
+        w_rows = [keep.tile([P, 2, C], BF16, name="w_rows%d" % b) for b in range(N_PIECES)]
+        for b in range(N_PIECES):
+            first_row = piece_first_row[b]
             nc.sync.dma_start(
-                out=w_tile[:],
-                in_=w[first_row : first_row + C, :].rearrange("(s p t) k -> p s t k", s=2, t=2),
+                out=w_rows[b][:],
+                in_=piece_weights[b][first_row : first_row + PIECE, :].rearrange(
+                    "(p t) k -> p t k", t=2
+                ),
             )
-            w_rows.append(w_tile)
-        for i, vector in enumerate((ln_k_g, ln_k_b, ln_v_g, ln_v_b)):
+            if b == 0:
+                nc.sync.dma_start(out=bias_rows[0:4, :], in_=bk.rearrange("(r c) -> r c", r=4))
+                nc.sync.dma_start(out=bias_rows[4:8, :], in_=bv.rearrange("(r c) -> r c", r=4))
+        for i, vector in enumerate((ln_v_g, ln_v_b, ln_k_g, ln_k_b)):
             nc.sync.dma_start(
                 out=affine_rows[2 * i : 2 * i + 2, :], in_=vector.rearrange("(r c) -> r c", r=2)
             )
         noise = keep.tile([P, C], BF16)
         nc.sync.dma_start(out=noise[:], in_=eps_noise.flatten_outer_dims())
-
-        bias_columns = rows_to_columns(nc, psum, small, bias_rows, 8, ident, "bias_columns")
-        bias_all = keep.tile([P, 2, 2 * C], BF16)
-        for i in range(2):
-            bank = psum.tile([P, BANK], F32, tag="words", name="bias_bank%d" % i)
-            repeat_on_all_partitions(nc, bank, bias_columns, 4 * i, ident)
-            if i == 0:
-                nc.scalar.copy(out=bias_all[:, i, :].bitcast(F32), in_=bank[:])
-            else:
-                nc.vector.tensor_copy(out=bias_all[:, i, :].bitcast(F32), in_=bank[:])
 
         ctx_bank = psum.tile([P, BANK], F32, tag="words")
         transpose_words(nc, ctx_bank, 0, ctx_rows[:], ident)
@@ -143,76 +122,162 @@ def tile_probcrossattention_pa_s_kernel(
             out=ctx_codes[:].bitcast(FP8X4), scales=ctx_scales[:], in_=ctx_grouped[:]
         )
 
-        x_var = work.tile([P, 2, C], F32)
-        x_mu = [work.tile([P, C], F32, name="x_mu%d" % i) for i in range(2)]
-        x_of_chunk = (x_var[:, 0, :], x_var[:, 1, :], x_mu[0][:], x_mu[1][:])
-        for i, (w, first_row, bias_row) in enumerate(chunks):
-            grouped = keep.tile([P, 4 * C], BF16, align_bytes=64, name="grouped%d" % i)
-            for s in range(2):
-                bank = psum.tile([P, BANK], F32, tag="words", name="w_bank%d_%d" % (i, s))
-                for t in range(2):
-                    transpose_words(nc, bank, 2 * P * t, w_rows[i][:, s, t, :], ident)
-                source = bank[:].rearrange("p (t u n) -> p n t u", t=2, u=2)
-                target = grouped[:].bitcast(F32)[:, BANK * s : BANK * (s + 1)].rearrange(
-                    "p (n t u) -> p n t u", t=2, u=2
-                )
-                if s == 0:
-                    nc.scalar.copy(out=target, in_=source)
-                else:
-                    nc.vector.tensor_copy(out=target, in_=source)
-            w_codes = keep.tile([P, C], U32, align_bytes=64, name="w_codes%d" % i)
-            w_scales = keep.tile([P, C], U8, align_bytes=64, name="w_scales%d" % i)
-            nc.vector.quantize_mx(
-                out=w_codes[:].bitcast(FP8X4), scales=w_scales[:], in_=grouped[:]
+        grouped = [
+            keep.tile([P, 4 * PIECE], BF16, align_bytes=64, name="grouped%d" % b)
+            for b in range(N_PIECES)
+        ]
+        w_codes = keep.tile([P, N_PIECES, PIECE], U32, align_bytes=64)
+        w_scales = keep.tile([P, N_PIECES, PIECE], U8, align_bytes=64)
+        bias_all = keep.tile([P, N_PIECES, PIECE], BF16)
+        x_all = keep.tile([P, N_PIECES, PIECE], F32)
+        ramp = keep.tile([P, N_VAR_PIECES, PIECE], F32)
+        shrunk = keep.tile([P, N_VAR_PIECES, PIECE], F32)
+        stats = small.tile([P, N_PIECES - N_VAR_PIECES, 6], F32)
+
+        def flip_and_group(b):
+            bank = psum.tile([P, BANK], F32, tag="words", name="w_bank%d" % b)
+            for t in range(2):
+                transpose_words(nc, bank, 2 * P * t, w_rows[b][:, t, :], ident)
+            nc.scalar.copy(
+                out=grouped[b][:].bitcast(F32).rearrange("p (n t u) -> p n t u", t=2, u=2),
+                in_=bank[:].rearrange("p (t u n) -> p n t u", t=2, u=2),
             )
-            acc = psum_acc.tile([P, C], F32)
+
+        def quantise(b):
+            nc.vector.quantize_mx(
+                out=w_codes[:, b, :].bitcast(FP8X4), scales=w_scales[:, b, :], in_=grouped[b][:]
+            )
+
+        def multiply_and_add_bias(b):
+            acc = psum_acc.tile([P, PIECE], F32, name="acc")
             nc.tensor.matmul_mx(
                 out=acc[:],
                 lhsT=ctx_codes[:].bitcast(FP8X4),
                 lhsT_scale=ctx_scales[:],
-                rhs=w_codes[:].bitcast(FP8X4),
-                rhs_scale=w_scales[:],
+                rhs=w_codes[:, b, :].bitcast(FP8X4),
+                rhs_scale=w_scales[:, b, :],
                 start=True,
                 stop=True,
             )
             nc.vector.tensor_tensor(
-                out=x_of_chunk[i], in0=acc[:],
-                in1=bias_all[:, bias_row, first_row : first_row + C], op=ALU.add,
+                out=x_all[:, b, :], in0=acc[:], in1=bias_all[:, b, :], op=ALU.add
             )
+            if b < N_VAR_PIECES:
+                nc.vector.tensor_scalar(
+                    out=ramp[:, b, :], in0=x_all[:, b, :], scalar1=0.0, scalar2=VAR_EPS,
+                    op0=ALU.max, op1=ALU.add,
+                )
+            else:
+                nc.vector.bn_stats(out=stats[:, b - N_VAR_PIECES, :], in_=x_all[:, b, :])
 
-        shrunk = work.tile([P, 2, C], F32)
-        for half in (V_VAR, K_VAR):
-            nc.scalar.activation(out=shrunk[:, half, :], in_=x_var[:, half, :], func=ACT.Abs)
+        def shrink(b):
+            nc.scalar.activation(out=shrunk[:, b, :], in_=x_all[:, b, :], func=ACT.Abs)
             nc.scalar.activation(
-                out=shrunk[:, half, :], in_=shrunk[:, half, :], func=ACT.Exp, scale=-1.0
+                out=shrunk[:, b, :], in_=shrunk[:, b, :], func=ACT.Exp, scale=-1.0
             )
-        ramp = work.tile([P, 2, C], F32)
-        nc.vector.tensor_scalar(
-            out=ramp[:], in0=x_var[:], scalar1=0.0, scalar2=VAR_EPS, op0=ALU.max, op1=ALU.add
-        )
-        log_term = work.tile([P, 2, C], F32)
-        nc.scalar.activation(out=log_term[:], in_=shrunk[:], func=ACT.Ln, bias=one[:, 0:1])
-        variance = work.tile([P, 2, C], F32)
-        nc.vector.tensor_tensor(out=variance[:], in0=ramp[:], in1=log_term[:], op=ALU.add)
-        nc.sync.dma_start(out=k_var_out, in_=variance[:, K_VAR, :])
-        v_std = work.tile([P, C], F32)
-        nc.scalar.activation(out=v_std[:], in_=variance[:, V_VAR, :], func=ACT.Sqrt)
 
+        def run_steps(first, last):
+            for step in range(first, last):
+                if step < N_PIECES:
+                    flip_and_group(step)
+                if 0 <= step - QUANTISE_LAG < N_PIECES:
+                    quantise(step - QUANTISE_LAG)
+                if 0 <= step - MULTIPLY_LAG < N_PIECES:
+                    multiply_and_add_bias(step - MULTIPLY_LAG)
+                if 0 <= step - EXP_LAG < N_VAR_PIECES:
+                    shrink(step - EXP_LAG)
+
+        def spread_biases(first_piece):
+            bank = psum.tile([P, BANK], F32, tag="words", name="bias_bank%d" % first_piece)
+            repeat_on_all_partitions(
+                nc, bank, bias_columns, piece_bias_row[first_piece : first_piece + 4], ident
+            )
+            nc.vector.tensor_copy(
+                out=bias_all[:, first_piece : first_piece + 4, :]
+                .rearrange("p b c -> p (b c)")
+                .bitcast(F32),
+                in_=bank[:],
+            )
+
+        def spread_affine(i, name):
+            bank = psum_affine.tile([P, BANK], F32, name=name)
+            repeat_on_all_partitions(nc, bank, affine_columns, range(4 * i, 4 * i + 4), ident)
+            return bank[:].bitcast(BF16)
+
+        def mean_and_rstd(i, name):
+            mean_var = small.tile([P, 2], F32, name=name + "_mean_var")
+            nc.vector.bn_aggr(
+                out=mean_var[:], in_=stats[:, 2 * i : 2 * i + 2, :].rearrange("p a b -> p (a b)")
+            )
+            rstd = small.tile([P, 1], F32, name=name + "_rstd")
+            nc.gpsimd.tensor_scalar(
+                out=rstd[:], in0=mean_var[:, 1:2], scalar1=LN_EPS, scalar2=None, op0=ALU.add
+            )
+            nc.gpsimd.tensor_tensor(out=rstd[:], in0=rstd[:], in1=minus_half[:], op=ALU.pow)
+            return mean_var, rstd
+
+        def centre_and_gain(i, mean_var, affine, name):
+            first = N_VAR_PIECES + 2 * i
+            centred = keep.tile([P, C], F32, name=name + "_centred")
+            nc.vector.scalar_tensor_tensor(
+                out=centred[:], in0=x_all[:, first : first + 2, :].rearrange("p b c -> p (b c)"),
+                scalar=mean_var[:, 0:1], in1=affine[:, 0:C], op0=ALU.subtract, op1=ALU.mult,
+            )
+            return centred
+
+        def scale_and_shift(centred, rstd, affine, name):
+            normed = keep.tile([P, C], F32, name=name + "_mu")
+            nc.vector.scalar_tensor_tensor(
+                out=normed[:], in0=centred[:], scalar=rstd[:, 0:1], in1=affine[:, C : 2 * C],
+                op0=ALU.mult, op1=ALU.add,
+            )
+            return normed
+
+        run_steps(0, 1)
+        bias_columns = rows_to_columns(nc, psum, small, bias_rows, 8, ident, "bias_columns")
+        run_steps(1, 3)
+        spread_biases(0)
+        run_steps(3, 6)
+        spread_biases(N_VAR_PIECES)
         affine_columns = rows_to_columns(nc, psum, small, affine_rows, 8, ident, "affine_columns")
-        affine = []
-        for i in range(2):
-            bank = psum_affine.tile([P, BANK], F32, name="affine_bank%d" % i)
-            repeat_on_all_partitions(nc, bank, affine_columns, 4 * i, ident)
-            affine.append(bank[:].bitcast(BF16))
+        run_steps(6, 8)
 
-        v_mu = layer_norm(
-            nc, work, small, x_mu[0], affine[1][:, 0:C], affine[1][:, C : 2 * C], minus_half, "v"
+        log_term = keep.tile([P, N_VAR_PIECES, PIECE], F32)
+        nc.scalar.activation(out=log_term[:], in_=shrunk[:], func=ACT.Ln, bias=one[:, 0:1])
+
+        run_steps(8, 9)
+        v_affine = spread_affine(0, "v_affine")
+        k_affine = spread_affine(1, "k_affine")
+        run_steps(9, N_PIECES + MULTIPLY_LAG)
+
+        v_mean_var, v_rstd = mean_and_rstd(0, "v")
+        k_mean_var, k_rstd = mean_and_rstd(1, "k")
+        v_centred = centre_and_gain(0, v_mean_var, v_affine, "v")
+        variance = keep.tile([P, 2, C], F32)
+        ramp_halves = ramp[:].rearrange("p (h b) c -> p h (b c)", h=2)
+        log_halves = log_term[:].rearrange("p (h b) c -> p h (b c)", h=2)
+        nc.vector.tensor_tensor(
+            out=variance[:, 0, :], in0=ramp_halves[:, 0, :], in1=log_halves[:, 0, :], op=ALU.add
         )
-        k_mu = layer_norm(
-            nc, work, small, x_mu[1], affine[0][:, 0:C], affine[0][:, C : 2 * C], minus_half, "k"
-        )
+        k_centred = centre_and_gain(1, k_mean_var, k_affine, "k")
+        v_mu = scale_and_shift(v_centred, v_rstd, v_affine, "v")
+        k_mu = scale_and_shift(k_centred, k_rstd, k_affine, "k")
         nc.sync.dma_start(out=k_mu_out, in_=k_mu[:])
-        v_sample = work.tile([P, C], F32)
-        nc.vector.tensor_tensor(out=v_sample[:], in0=v_std[:], in1=noise[:], op=ALU.mult)
-        nc.vector.tensor_tensor(out=v_sample[:], in0=v_sample[:], in1=v_mu[:], op=ALU.add)
-        nc.sync.dma_start(out=v_sample_out, in_=v_sample[:])
+        nc.gpsimd.tensor_tensor(
+            out=variance[:, 1, :], in0=ramp_halves[:, 1, :], in1=log_halves[:, 1, :], op=ALU.add
+        )
+        nc.sync.dma_start(out=k_var_out, in_=variance[:, 1, :])
+
+        v_std = keep.tile([P, C], F32)
+        v_sample = keep.tile([P, C], F32)
+        halves = (slice(0, C // 2), slice(C // 2, C))
+        for cols in halves:
+            nc.scalar.activation(out=v_std[:, cols], in_=variance[:, 0, cols], func=ACT.Sqrt)
+        for cols in halves:
+            nc.vector.tensor_tensor(
+                out=v_sample[:, cols], in0=v_std[:, cols], in1=noise[:, cols], op=ALU.mult
+            )
+            nc.vector.tensor_tensor(
+                out=v_sample[:, cols], in0=v_sample[:, cols], in1=v_mu[:, cols], op=ALU.add
+            )
+            nc.sync.dma_start(out=v_sample_out[:, cols], in_=v_sample[:, cols])

@@ -16,13 +16,13 @@ C = 512
 BANK = 512
 PIECE = 256
 N_PIECES = 4 * C // PIECE
-N_VAR_PIECES = N_PIECES // 2
+V_VAR, K_VAR, V_MU, K_MU = 0, 1, 2, 3
 VAR_EPS = 1e-6
 LN_EPS = 1e-5
 
 QUANTISE_LAG = 1
-MULTIPLY_LAG = 3
-EXP_LAG = 4
+MULTIPLY_LAG = 4
+EXP_LAG = 6
 
 FLOPS = 2 * P * C * 4 * C
 
@@ -52,6 +52,13 @@ def repeat_on_all_partitions(nc, bank, columns, four_rows, ident):
         )
 
 
+def quarter_due(step, lag):
+    piece = step - lag
+    if 0 <= piece < N_PIECES and piece % 2 == 1:
+        return piece // 2
+    return None
+
+
 def tile_probcrossattention_pa_s_kernel(
     tc, context, eps_noise, Wk, bk, Wv, bv, ln_k_g, ln_k_b, ln_v_g, ln_v_b, out_0, out_1, out_2
 ):
@@ -60,14 +67,9 @@ def tile_probcrossattention_pa_s_kernel(
     k_var_out = out_1.flatten_outer_dims()
     v_sample_out = out_2.flatten_outer_dims()
 
-    piece_weights = []
-    piece_first_row = []
-    piece_bias_row = []
-    for w, bias_base, half in ((Wv, 4, 1), (Wk, 0, 1), (Wv, 4, 0), (Wk, 0, 0)):
-        for s in range(2):
-            piece_weights.append(w)
-            piece_first_row.append(C * half + PIECE * s)
-            piece_bias_row.append(bias_base + 2 * half + s)
+    quarter_weights = (Wv, Wk, Wv, Wk)
+    quarter_first_row = (C, C, 0, 0)
+    quarter_bias_row = (6, 2, 4, 0)
 
     with ExitStack() as stack:
         stack.enter_context(tc.manual_schedule())
@@ -85,6 +87,8 @@ def tile_probcrossattention_pa_s_kernel(
         nc.vector.memset(affine_rows[:], 0.0)
         one = small.tile([P, 1], F32)
         nc.vector.memset(one[:], 1.0)
+        var_eps = small.tile([P, 1], F32)
+        nc.vector.memset(var_eps[:], VAR_EPS)
         minus_half = small.tile([P, 1], F32)
         nc.vector.memset(minus_half[:], -0.5)
 
@@ -92,10 +96,10 @@ def tile_probcrossattention_pa_s_kernel(
         nc.sync.dma_start(out=ctx_rows[:], in_=context.flatten_outer_dims())
         w_rows = [keep.tile([P, 2, C], BF16, name="w_rows%d" % b) for b in range(N_PIECES)]
         for b in range(N_PIECES):
-            first_row = piece_first_row[b]
+            first_row = quarter_first_row[b // 2] + PIECE * (b % 2)
             nc.sync.dma_start(
                 out=w_rows[b][:],
-                in_=piece_weights[b][first_row : first_row + PIECE, :].rearrange(
+                in_=quarter_weights[b // 2][first_row : first_row + PIECE, :].rearrange(
                     "(p t) k -> p t k", t=2
                 ),
             )
@@ -126,75 +130,77 @@ def tile_probcrossattention_pa_s_kernel(
             keep.tile([P, 4 * PIECE], BF16, align_bytes=64, name="grouped%d" % b)
             for b in range(N_PIECES)
         ]
-        w_codes = keep.tile([P, N_PIECES, PIECE], U32, align_bytes=64)
-        w_scales = keep.tile([P, N_PIECES, PIECE], U8, align_bytes=64)
-        bias_all = keep.tile([P, N_PIECES, PIECE], BF16)
-        x_all = keep.tile([P, N_PIECES, PIECE], F32)
-        ramp = keep.tile([P, N_VAR_PIECES, PIECE], F32)
-        shrunk = keep.tile([P, N_VAR_PIECES, PIECE], F32)
-        stats = small.tile([P, N_PIECES - N_VAR_PIECES, 6], F32)
+        w_codes = keep.tile([P, 4, C], U32, align_bytes=64)
+        w_scales = keep.tile([P, 4, C], U8, align_bytes=64)
+        bias_all = keep.tile([P, 4, C], BF16)
+        x_all = keep.tile([P, 4, C], F32)
+        shrunk = keep.tile([P, 2, C], F32)
+        stats = small.tile([P, 2, 6], F32)
 
         def flip_and_group(b):
             bank = psum.tile([P, BANK], F32, tag="words", name="w_bank%d" % b)
             for t in range(2):
                 transpose_words(nc, bank, 2 * P * t, w_rows[b][:, t, :], ident)
-            nc.scalar.copy(
-                out=grouped[b][:].bitcast(F32).rearrange("p (n t u) -> p n t u", t=2, u=2),
-                in_=bank[:].rearrange("p (t u n) -> p n t u", t=2, u=2),
-            )
+            source = bank[:].rearrange("p (t u n) -> p n t u", t=2, u=2)
+            target = grouped[b][:].bitcast(F32).rearrange("p (n t u) -> p n t u", t=2, u=2)
+            if b % 4 < 3:
+                nc.scalar.copy(out=target, in_=source)
+            else:
+                nc.vector.tensor_copy(out=target, in_=source)
 
         def quantise(b):
+            cols = slice(PIECE * (b % 2), PIECE * (b % 2 + 1))
             nc.vector.quantize_mx(
-                out=w_codes[:, b, :].bitcast(FP8X4), scales=w_scales[:, b, :], in_=grouped[b][:]
+                out=w_codes[:, b // 2, cols].bitcast(FP8X4),
+                scales=w_scales[:, b // 2, cols],
+                in_=grouped[b][:],
             )
 
-        def multiply_and_add_bias(b):
-            acc = psum_acc.tile([P, PIECE], F32, name="acc")
+        def multiply_and_add_bias(quarter):
+            acc = psum_acc.tile([P, C], F32, name="acc")
             nc.tensor.matmul_mx(
                 out=acc[:],
                 lhsT=ctx_codes[:].bitcast(FP8X4),
                 lhsT_scale=ctx_scales[:],
-                rhs=w_codes[:, b, :].bitcast(FP8X4),
-                rhs_scale=w_scales[:, b, :],
+                rhs=w_codes[:, quarter, :].bitcast(FP8X4),
+                rhs_scale=w_scales[:, quarter, :],
                 start=True,
                 stop=True,
             )
             nc.vector.tensor_tensor(
-                out=x_all[:, b, :], in0=acc[:], in1=bias_all[:, b, :], op=ALU.add
+                out=x_all[:, quarter, :], in0=acc[:], in1=bias_all[:, quarter, :], op=ALU.add
             )
-            if b < N_VAR_PIECES:
-                nc.vector.tensor_scalar(
-                    out=ramp[:, b, :], in0=x_all[:, b, :], scalar1=0.0, scalar2=VAR_EPS,
-                    op0=ALU.max, op1=ALU.add,
-                )
-            else:
-                nc.vector.bn_stats(out=stats[:, b - N_VAR_PIECES, :], in_=x_all[:, b, :])
+            if quarter >= V_MU:
+                nc.vector.bn_stats(out=stats[:, quarter - V_MU, :], in_=x_all[:, quarter, :])
 
-        def shrink(b):
-            nc.scalar.activation(out=shrunk[:, b, :], in_=x_all[:, b, :], func=ACT.Abs)
+        def shrink(quarter):
+            nc.scalar.activation(out=shrunk[:, quarter, :], in_=x_all[:, quarter, :], func=ACT.Abs)
             nc.scalar.activation(
-                out=shrunk[:, b, :], in_=shrunk[:, b, :], func=ACT.Exp, scale=-1.0
+                out=shrunk[:, quarter, :], in_=shrunk[:, quarter, :], func=ACT.Exp, scale=-1.0
             )
 
         def run_steps(first, last):
             for step in range(first, last):
-                if step < N_PIECES:
-                    flip_and_group(step)
+                quarter = quarter_due(step, EXP_LAG)
+                if quarter is not None and quarter < V_MU:
+                    shrink(quarter)
+                quarter = quarter_due(step, MULTIPLY_LAG)
+                if quarter is not None:
+                    multiply_and_add_bias(quarter)
                 if 0 <= step - QUANTISE_LAG < N_PIECES:
                     quantise(step - QUANTISE_LAG)
-                if 0 <= step - MULTIPLY_LAG < N_PIECES:
-                    multiply_and_add_bias(step - MULTIPLY_LAG)
-                if 0 <= step - EXP_LAG < N_VAR_PIECES:
-                    shrink(step - EXP_LAG)
+                if step < N_PIECES:
+                    flip_and_group(step)
 
-        def spread_biases(first_piece):
-            bank = psum.tile([P, BANK], F32, tag="words", name="bias_bank%d" % first_piece)
-            repeat_on_all_partitions(
-                nc, bank, bias_columns, piece_bias_row[first_piece : first_piece + 4], ident
-            )
+        def spread_biases(first_quarter):
+            four_rows = []
+            for quarter in (first_quarter, first_quarter + 1):
+                four_rows.extend((quarter_bias_row[quarter], quarter_bias_row[quarter] + 1))
+            bank = psum.tile([P, BANK], F32, tag="words", name="bias_bank%d" % first_quarter)
+            repeat_on_all_partitions(nc, bank, bias_columns, four_rows, ident)
             nc.vector.tensor_copy(
-                out=bias_all[:, first_piece : first_piece + 4, :]
-                .rearrange("p b c -> p (b c)")
+                out=bias_all[:, first_quarter : first_quarter + 2, :]
+                .rearrange("p q c -> p (q c)")
                 .bitcast(F32),
                 in_=bank[:],
             )
@@ -204,11 +210,9 @@ def tile_probcrossattention_pa_s_kernel(
             repeat_on_all_partitions(nc, bank, affine_columns, range(4 * i, 4 * i + 4), ident)
             return bank[:].bitcast(BF16)
 
-        def mean_and_rstd(i, name):
+        def mean_and_rstd(quarter, name):
             mean_var = small.tile([P, 2], F32, name=name + "_mean_var")
-            nc.vector.bn_aggr(
-                out=mean_var[:], in_=stats[:, 2 * i : 2 * i + 2, :].rearrange("p a b -> p (a b)")
-            )
+            nc.vector.bn_aggr(out=mean_var[:], in_=stats[:, quarter - V_MU, :])
             rstd = small.tile([P, 1], F32, name=name + "_rstd")
             nc.gpsimd.tensor_scalar(
                 out=rstd[:], in0=mean_var[:, 1:2], scalar1=LN_EPS, scalar2=None, op0=ALU.add
@@ -216,12 +220,11 @@ def tile_probcrossattention_pa_s_kernel(
             nc.gpsimd.tensor_tensor(out=rstd[:], in0=rstd[:], in1=minus_half[:], op=ALU.pow)
             return mean_var, rstd
 
-        def centre_and_gain(i, mean_var, affine, name):
-            first = N_VAR_PIECES + 2 * i
+        def centre_and_gain(quarter, mean_var, affine, name):
             centred = keep.tile([P, C], F32, name=name + "_centred")
             nc.vector.scalar_tensor_tensor(
-                out=centred[:], in0=x_all[:, first : first + 2, :].rearrange("p b c -> p (b c)"),
-                scalar=mean_var[:, 0:1], in1=affine[:, 0:C], op0=ALU.subtract, op1=ALU.mult,
+                out=centred[:], in0=x_all[:, quarter, :], scalar=mean_var[:, 0:1],
+                in1=affine[:, 0:C], op0=ALU.subtract, op1=ALU.mult,
             )
             return centred
 
@@ -236,43 +239,46 @@ def tile_probcrossattention_pa_s_kernel(
         run_steps(0, 1)
         bias_columns = rows_to_columns(nc, psum, small, bias_rows, 8, ident, "bias_columns")
         run_steps(1, 3)
-        spread_biases(0)
-        run_steps(3, 6)
-        spread_biases(N_VAR_PIECES)
+        spread_biases(V_VAR)
+        run_steps(3, N_PIECES + 1)
+        spread_biases(V_MU)
         affine_columns = rows_to_columns(nc, psum, small, affine_rows, 8, ident, "affine_columns")
-        run_steps(6, 8)
+        run_steps(N_PIECES + 1, K_VAR * 2 + 1 + EXP_LAG + 1)
 
-        log_term = keep.tile([P, N_VAR_PIECES, PIECE], F32)
+        log_term = keep.tile([P, 2, C], F32)
         nc.scalar.activation(out=log_term[:], in_=shrunk[:], func=ACT.Ln, bias=one[:, 0:1])
+        k_var = keep.tile([P, C], F32)
+        nc.gpsimd.tensor_scalar(
+            out=k_var[:], in0=x_all[:, K_VAR, :], scalar1=0.0, scalar2=VAR_EPS,
+            op0=ALU.max, op1=ALU.add,
+        )
 
-        run_steps(8, 9)
+        run_steps(K_VAR * 2 + 1 + EXP_LAG + 1, N_PIECES + MULTIPLY_LAG)
         v_affine = spread_affine(0, "v_affine")
         k_affine = spread_affine(1, "k_affine")
-        run_steps(9, N_PIECES + MULTIPLY_LAG)
 
-        v_mean_var, v_rstd = mean_and_rstd(0, "v")
-        k_mean_var, k_rstd = mean_and_rstd(1, "k")
-        v_centred = centre_and_gain(0, v_mean_var, v_affine, "v")
-        variance = keep.tile([P, 2, C], F32)
-        ramp_halves = ramp[:].rearrange("p (h b) c -> p h (b c)", h=2)
-        log_halves = log_term[:].rearrange("p (h b) c -> p h (b c)", h=2)
-        nc.vector.tensor_tensor(
-            out=variance[:, 0, :], in0=ramp_halves[:, 0, :], in1=log_halves[:, 0, :], op=ALU.add
+        v_mean_var, v_rstd = mean_and_rstd(V_MU, "v")
+        k_mean_var, k_rstd = mean_and_rstd(K_MU, "k")
+        v_centred = centre_and_gain(V_MU, v_mean_var, v_affine, "v")
+        v_softplus = keep.tile([P, C], F32)
+        nc.vector.scalar_tensor_tensor(
+            out=v_softplus[:], in0=x_all[:, V_VAR, :], scalar=0.0, in1=log_term[:, V_VAR, :],
+            op0=ALU.max, op1=ALU.add,
         )
-        k_centred = centre_and_gain(1, k_mean_var, k_affine, "k")
+        k_centred = centre_and_gain(K_MU, k_mean_var, k_affine, "k")
         v_mu = scale_and_shift(v_centred, v_rstd, v_affine, "v")
         k_mu = scale_and_shift(k_centred, k_rstd, k_affine, "k")
         nc.sync.dma_start(out=k_mu_out, in_=k_mu[:])
-        nc.gpsimd.tensor_tensor(
-            out=variance[:, 1, :], in0=ramp_halves[:, 1, :], in1=log_halves[:, 1, :], op=ALU.add
-        )
-        nc.sync.dma_start(out=k_var_out, in_=variance[:, 1, :])
+        nc.gpsimd.tensor_tensor(out=k_var[:], in0=k_var[:], in1=log_term[:, K_VAR, :], op=ALU.add)
+        nc.sync.dma_start(out=k_var_out, in_=k_var[:])
 
         v_std = keep.tile([P, C], F32)
         v_sample = keep.tile([P, C], F32)
         halves = (slice(0, C // 2), slice(C // 2, C))
         for cols in halves:
-            nc.scalar.activation(out=v_std[:, cols], in_=variance[:, 0, cols], func=ACT.Sqrt)
+            nc.scalar.activation(
+                out=v_std[:, cols], in_=v_softplus[:, cols], func=ACT.Sqrt, bias=var_eps[:, 0:1]
+            )
         for cols in halves:
             nc.vector.tensor_tensor(
                 out=v_sample[:, cols], in0=v_std[:, cols], in1=noise[:, cols], op=ALU.mult

@@ -240,8 +240,8 @@ def tile_probcrossattention_pa_s_kernel(
         bias_columns = rows_to_columns(nc, psum, small, bias_rows, 8, ident, "bias_columns")
         run_steps(1, 3)
         spread_biases(V_VAR)
-        run_steps(3, N_PIECES + 1)
         spread_biases(V_MU)
+        run_steps(3, N_PIECES + 1)
         affine_columns = rows_to_columns(nc, psum, small, affine_rows, 8, ident, "affine_columns")
         run_steps(N_PIECES + 1, K_VAR * 2 + 1 + EXP_LAG + 1)
 

from contextlib import ExitStack

import concourse.mybir as mybir
from concourse.masks import make_identity

F32 = mybir.dt.float32
BF16 = mybir.dt.bfloat16
U32 = mybir.dt.uint32
U8 = mybir.dt.uint8
FP8X4 = mybir.dt.float8_e4m3fn_x4
ALU = mybir.AluOpType
ACT = mybir.ActivationFunctionType

P = 128
C = 512
BANK = 512
PIECE = 256
N_PIECES = 4 * C // PIECE
V_VAR, K_VAR, V_MU, K_MU = 0, 1, 2, 3
VAR_EPS = 1e-6
LN_EPS = 1e-5

QUANTISE_LAG = 1
MULTIPLY_LAG = 4
EXP_LAG = 6

FLOPS = 2 * P * C * 4 * C


def transpose_words(nc, bank, first_column, rows_bf16, ident):
    words = rows_bf16.bitcast(F32)
    for u in range(2):
        nc.tensor.transpose(
            bank[:, first_column + P * u : first_column + P * (u + 1)],
            words[:, P * u : P * (u + 1)],
            ident[:],
        )


def rows_to_columns(nc, psum, small, rows, n_rows, ident, name):
    flipped = psum.tile([P, BANK], F32, tag="words", name=name + "_flipped")
    nc.tensor.transpose(flipped[:, 0:P], rows[:].bitcast(F32), ident[:])
    columns = small.tile([P, n_rows], F32, name=name)
    nc.vector.tensor_copy(out=columns[:], in_=flipped[:, 0:n_rows])
    return columns


def repeat_on_all_partitions(nc, bank, columns, four_rows, ident):
    for i, r in enumerate(four_rows):
        nc.tensor.transpose(
            bank[:, P * i : P * (i + 1)], columns[:, r : r + 1].to_broadcast([P, P]), ident[:]
        )


def quarter_due(step, lag):
    piece = step - lag
    if 0 <= piece < N_PIECES and piece % 2 == 1:
        return piece // 2
    return None


def tile_probcrossattention_pa_s_kernel(
    tc, context, eps_noise, Wk, bk, Wv, bv, ln_k_g, ln_k_b, ln_v_g, ln_v_b, out_0, out_1, out_2
):
    nc = tc.nc
    k_mu_out = out_0.flatten_outer_dims()
    k_var_out = out_1.flatten_outer_dims()
    v_sample_out = out_2.flatten_outer_dims()

    quarter_weights = (Wv, Wk, Wv, Wk)
    quarter_first_row = (C, C, 0, 0)
    quarter_bias_row = (6, 2, 4, 0)

    with ExitStack() as stack:
        stack.enter_context(tc.manual_schedule())
        keep = stack.enter_context(tc.tile_pool(name="keep", bufs=1))
        small = stack.enter_context(tc.tile_pool(name="small", bufs=1))
        psum = stack.enter_context(tc.psum_pool(name="psum", bufs=4))
        psum_acc = stack.enter_context(tc.psum_pool(name="psum_acc", bufs=2))
        psum_affine = stack.enter_context(tc.psum_pool(name="psum_affine", bufs=1))

        ident = keep.tile([P, P], F32)
        make_identity(nc, ident[:])
        bias_rows = keep.tile([P, 2 * P], BF16)
        nc.vector.memset(bias_rows[:], 0.0)
        affine_rows = keep.tile([P, 2 * P], BF16)
        nc.vector.memset(affine_rows[:], 0.0)
        one = small.tile([P, 1], F32)
        nc.vector.memset(one[:], 1.0)
        var_eps = small.tile([P, 1], F32)
        nc.vector.memset(var_eps[:], VAR_EPS)
        minus_half = small.tile([P, 1], F32)
        nc.vector.memset(minus_half[:], -0.5)

        ctx_rows = keep.tile([P, C], BF16)
        nc.sync.dma_start(out=ctx_rows[:], in_=context.flatten_outer_dims())
        w_rows = [keep.tile([P, 2, C], BF16, name="w_rows%d" % b) for b in range(N_PIECES)]
        for b in range(N_PIECES):
            first_row = quarter_first_row[b // 2] + PIECE * (b % 2)
            nc.sync.dma_start(
                out=w_rows[b][:],
                in_=quarter_weights[b // 2][first_row : first_row + PIECE, :].rearrange(
                    "(p t) k -> p t k", t=2
                ),
            )
            if b == 0:
                nc.sync.dma_start(out=bias_rows[0:4, :], in_=bk.rearrange("(r c) -> r c", r=4))
                nc.sync.dma_start(out=bias_rows[4:8, :], in_=bv.rearrange("(r c) -> r c", r=4))
        for i, vector in enumerate((ln_v_g, ln_v_b, ln_k_g, ln_k_b)):
            nc.sync.dma_start(
                out=affine_rows[2 * i : 2 * i + 2, :], in_=vector.rearrange("(r c) -> r c", r=2)
            )
        noise = keep.tile([P, C], BF16)
        nc.sync.dma_start(out=noise[:], in_=eps_noise.flatten_outer_dims())

        ctx_bank = psum.tile([P, BANK], F32, tag="words")
        transpose_words(nc, ctx_bank, 0, ctx_rows[:], ident)
        ctx_grouped = keep.tile([P, 4 * P], BF16, align_bytes=64)
        nc.vector.tensor_copy(
            out=ctx_grouped[:].bitcast(F32).rearrange("p (n u) -> p n u", u=2),
            in_=ctx_bank[:, 0 : 2 * P].rearrange("p (u n) -> p n u", u=2),
        )
        ctx_codes = keep.tile([P, P], U32, align_bytes=64)
        ctx_scales = keep.tile([P, P], U8, align_bytes=64)
        nc.vector.quantize_mx(
            out=ctx_codes[:].bitcast(FP8X4), scales=ctx_scales[:], in_=ctx_grouped[:]
        )

        grouped = [
            keep.tile([P, 4 * PIECE], BF16, align_bytes=64, name="grouped%d" % b)
            for b in range(N_PIECES)
        ]
        w_codes = keep.tile([P, 4, C], U32, align_bytes=64)
        w_scales = keep.tile([P, 4, C], U8, align_bytes=64)
        bias_all = keep.tile([P, 4, C], BF16)
        x_all = keep.tile([P, 4, C], F32)
        shrunk = keep.tile([P, 2, C], F32)
        stats = small.tile([P, 2, 6], F32)

        def flip_and_group(b):
            bank = psum.tile([P, BANK], F32, tag="words", name="w_bank%d" % b)
            for t in range(2):
                transpose_words(nc, bank, 2 * P * t, w_rows[b][:, t, :], ident)
            source = bank[:].rearrange("p (t u n) -> p n t u", t=2, u=2)
            target = grouped[b][:].bitcast(F32).rearrange("p (n t u) -> p n t u", t=2, u=2)
            if b % 4 < 3:
                nc.scalar.copy(out=target, in_=source)
            else:
                nc.vector.tensor_copy(out=target, in_=source)

        def quantise(b):
            cols = slice(PIECE * (b % 2), PIECE * (b % 2 + 1))
            nc.vector.quantize_mx(
                out=w_codes[:, b // 2, cols].bitcast(FP8X4),
                scales=w_scales[:, b // 2, cols],
                in_=grouped[b][:],
            )

        def multiply_and_add_bias(quarter):
            acc = psum_acc.tile([P, C], F32, name="acc")
            nc.tensor.matmul_mx(
                out=acc[:],
                lhsT=ctx_codes[:].bitcast(FP8X4),
                lhsT_scale=ctx_scales[:],
                rhs=w_codes[:, quarter, :].bitcast(FP8X4),
                rhs_scale=w_scales[:, quarter, :],
                start=True,
                stop=True,
            )
            nc.vector.tensor_tensor(
                out=x_all[:, quarter, :], in0=acc[:], in1=bias_all[:, quarter, :], op=ALU.add
            )
            if quarter >= V_MU:
                nc.vector.bn_stats(out=stats[:, quarter - V_MU, :], in_=x_all[:, quarter, :])

        def shrink(quarter):
            nc.scalar.activation(out=shrunk[:, quarter, :], in_=x_all[:, quarter, :], func=ACT.Abs)
            nc.scalar.activation(
                out=shrunk[:, quarter, :], in_=shrunk[:, quarter, :], func=ACT.Exp, scale=-1.0
            )

        def run_steps(first, last):
            for step in range(first, last):
                quarter = quarter_due(step, EXP_LAG)
                if quarter is not None and quarter < V_MU:
                    shrink(quarter)
                quarter = quarter_due(step, MULTIPLY_LAG)
                if quarter is not None:
                    multiply_and_add_bias(quarter)
                if 0 <= step - QUANTISE_LAG < N_PIECES:
                    quantise(step - QUANTISE_LAG)
                if step < N_PIECES:
                    flip_and_group(step)

        def spread_biases(first_quarter):
            four_rows = []
            for quarter in (first_quarter, first_quarter + 1):
                four_rows.extend((quarter_bias_row[quarter], quarter_bias_row[quarter] + 1))
            bank = psum.tile([P, BANK], F32, tag="words", name="bias_bank%d" % first_quarter)
            repeat_on_all_partitions(nc, bank, bias_columns, four_rows, ident)
            nc.vector.tensor_copy(
                out=bias_all[:, first_quarter : first_quarter + 2, :]
                .rearrange("p q c -> p (q c)")
                .bitcast(F32),
                in_=bank[:],
            )

        def spread_affine(i, name):
            bank = psum_affine.tile([P, BANK], F32, name=name)
            repeat_on_all_partitions(nc, bank, affine_columns, range(4 * i, 4 * i + 4), ident)
            return bank[:].bitcast(BF16)

        def mean_and_rstd(quarter, name):
            mean_var = small.tile([P, 2], F32, name=name + "_mean_var")
            nc.vector.bn_aggr(out=mean_var[:], in_=stats[:, quarter - V_MU, :])
            rstd = small.tile([P, 1], F32, name=name + "_rstd")
            nc.gpsimd.tensor_scalar(
                out=rstd[:], in0=mean_var[:, 1:2], scalar1=LN_EPS, scalar2=None, op0=ALU.add
            )
            nc.gpsimd.tensor_tensor(out=rstd[:], in0=rstd[:], in1=minus_half[:], op=ALU.pow)
            return mean_var, rstd

        def centre_and_gain(quarter, mean_var, affine, name):
            centred = keep.tile([P, C], F32, name=name + "_centred")
            nc.vector.scalar_tensor_tensor(
                out=centred[:], in0=x_all[:, quarter, :], scalar=mean_var[:, 0:1],
                in1=affine[:, 0:C], op0=ALU.subtract, op1=ALU.mult,
            )
            return centred

        def scale_and_shift(centred, rstd, affine, name):
            normed = keep.tile([P, C], F32, name=name + "_mu")
            nc.vector.scalar_tensor_tensor(
                out=normed[:], in0=centred[:], scalar=rstd[:, 0:1], in1=affine[:, C : 2 * C],
                op0=ALU.mult, op1=ALU.add,
            )
            return normed

        run_steps(0, 1)
        bias_columns = rows_to_columns(nc, psum, small, bias_rows, 8, ident, "bias_columns")
        run_steps(1, 3)
        spread_biases(V_VAR)
        spread_biases(V_MU)
        run_steps(3, N_PIECES + 1)
        affine_columns = rows_to_columns(nc, psum, small, affine_rows, 8, ident, "affine_columns")
        run_steps(N_PIECES + 1, K_VAR * 2 + 1 + EXP_LAG + 1)

        log_term = keep.tile([P, 2, C], F32)
        nc.scalar.activation(out=log_term[:], in_=shrunk[:], func=ACT.Ln, bias=one[:, 0:1])
        k_var = keep.tile([P, C], F32)
        nc.gpsimd.tensor_scalar(
            out=k_var[:], in0=x_all[:, K_VAR, :], scalar1=0.0, scalar2=VAR_EPS,
            op0=ALU.max, op1=ALU.add,
        )

        run_steps(K_VAR * 2 + 1 + EXP_LAG + 1, N_PIECES + MULTIPLY_LAG)
        v_affine = spread_affine(0, "v_affine")
        k_affine = spread_affine(1, "k_affine")

        v_mean_var, v_rstd = mean_and_rstd(V_MU, "v")
        k_mean_var, k_rstd = mean_and_rstd(K_MU, "k")
        v_centred = centre_and_gain(V_MU, v_mean_var, v_affine, "v")
        v_softplus = keep.tile([P, C], F32)
        nc.vector.scalar_tensor_tensor(
            out=v_softplus[:], in0=x_all[:, V_VAR, :], scalar=0.0, in1=log_term[:, V_VAR, :],
            op0=ALU.max, op1=ALU.add,
        )
        k_centred = centre_and_gain(K_MU, k_mean_var, k_affine, "k")
        v_mu = scale_and_shift(v_centred, v_rstd, v_affine, "v")
        k_mu = scale_and_shift(k_centred, k_rstd, k_affine, "k")
        nc.sync.dma_start(out=k_mu_out, in_=k_mu[:])
        nc.gpsimd.tensor_tensor(out=k_var[:], in0=k_var[:], in1=log_term[:, K_VAR, :], op=ALU.add)
        nc.sync.dma_start(out=k_var_out, in_=k_var[:])

        v_std = keep.tile([P, C], F32)
        v_sample = keep.tile([P, C], F32)
        halves = (slice(0, C // 2), slice(C // 2, C))
        for cols in halves:
            nc.scalar.activation(
                out=v_std[:, cols], in_=v_softplus[:, cols], func=ACT.Sqrt, bias=var_eps[:, 0:1]
            )
        for cols in halves:
            nc.vector.tensor_tensor(
                out=v_sample[:, cols], in0=v_std[:, cols], in1=noise[:, cols], op=ALU.mult
            )
            nc.vector.tensor_tensor(
                out=v_sample[:, cols], in0=v_sample[:, cols], in1=v_mu[:, cols], op=ALU.add
            )
            nc.sync.dma_start(out=v_sample_out[:, cols], in_=v_sample[:, cols])
